import numpy as np
import ml_dtypes


def mxq(x, axis, fmt="e4m3"):
    dtype, down = {"e4m3": (ml_dtypes.float8_e4m3fn, 7), "e5m2": (ml_dtypes.float8_e5m2, 14)}[fmt]
    v = np.moveaxis(np.asarray(x, np.float32).astype(ml_dtypes.bfloat16).astype(np.float64), axis, -1)
    blocks = v.reshape(v.shape[:-1] + (-1, 32))
    amax = np.abs(blocks).max(-1, keepdims=True)
    byte = np.maximum(np.where(amax > 0, np.frexp(amax)[1] - 1 + 127, 0) - down, 1)
    scale = np.exp2(byte - 127.0)
    codes = (blocks / scale).astype(np.float32).astype(dtype).astype(np.float64)
    return np.moveaxis((codes * scale).reshape(v.shape), -1, axis)


WIDE = False


def mx_kscale(k):
    if not WIDE:
        return np.ones(k)
    levels = np.array([10, -10, 5, -5, 0])
    if k % 512:
        return np.exp2(np.random.permutation(np.resize(levels, k // 32))).repeat(32)
    a = np.empty((k // 512, 16))
    for p in range(k // 512):
        a[p, :8] = np.random.permutation(np.resize(levels, 8))
        for g in range(8):
            far = levels[np.abs(levels - a[p, g]) >= 10]
            a[p, g + 8] = far[np.random.randint(len(far))]
    return np.exp2(a.ravel()).repeat(32)


BF16 = ml_dtypes.bfloat16


def bf(x):
    return np.asarray(x, np.float32).astype(BF16)


def f64(x):
    return np.asarray(x).astype(np.float64)


B, S, D, P, N1, N2, N3 = 2, 512, 1024, 128, 3, 2, 3
H = N1 + N2 + N3


def setup_inputs():
    s = mx_kscale(D)
    a = 1.0 / np.sqrt(D)
    return {"x": bf(np.random.standard_normal((B, S, D)) * s),
            "w_now": bf(np.random.standard_normal((H, P, D)) * a / s),
            "w_back1": bf(np.random.standard_normal((N2 + N3, P, D)) * a / s),
            "w_back2": bf(np.random.standard_normal((N3, P, D)) * a / s),
            "bias": bf(np.random.standard_normal((H, P)) * 0.5)}


def core(x, w_now, w_back1, w_back2, bias):
    xq = mxq(f64(x), 2, "e4m3")
    y = 0.0
    for j, w in enumerate((w_now, w_back1, w_back2)):
        z = xq @ mxq(f64(w), 2, "e4m3").reshape(-1, D).T
        y = y + np.pad(z[:, :S - j], ((0, 0), (j, 0), (H * P - z.shape[-1], 0)))
    return y.reshape(B, S, H, P).transpose(0, 2, 1, 3) + f64(bias)[None, :, None, :]


def e4m3fn_bytes(y):
    return np.clip(np.asarray(y, np.float64), -448.0, 448.0).astype(np.float32).astype(ml_dtypes.float8_e4m3fn).view(np.uint8)


Y_SCALE = 140.0


def reference(x, w_now, w_back1, w_back2, bias):
    out = core(x, w_now, w_back1, w_back2, bias)
    return out, e4m3fn_bytes(out * Y_SCALE)

@@ -1,0 +1,258 @@
+from contextlib import ExitStack
+
+import concourse.mybir as mybir
+from concourse.masks import make_identity
+
+B, S, D, P, H = 2, 512, 1024, 128, 8
+FLOPS = 2 * B * S * D * P * 16
+
+F32 = mybir.dt.float32
+BF16 = mybir.dt.bfloat16
+I32 = mybir.dt.int32
+U8 = mybir.dt.uint8
+FP8X4 = mybir.dt.float8_e4m3fn_x4
+FP8 = mybir.dt.float8_e4m3fn
+ALU = mybir.AluOpType
+ACT = mybir.ActivationFunctionType
+
+Y_SCALE = 140.0
+MANUAL = True
+
+
+def tile_multiheadhomogeneousattention_pa_kernel(tc, x, w_now, w_back1, w_back2, bias, out_0, out_1):
+    nc = tc.nc
+    with ExitStack() as ctx:
+        const = ctx.enter_context(tc.tile_pool(name="const", bufs=1))
+        raw = ctx.enter_context(tc.tile_pool(name="raw", bufs=1))
+        codes = ctx.enter_context(tc.tile_pool(name="codes", bufs=1))
+        grp = ctx.enter_context(tc.tile_pool(name="grp", bufs=3))
+        outp = ctx.enter_context(tc.tile_pool(name="outp", bufs=4))
+        f8p = ctx.enter_context(tc.tile_pool(name="f8p", bufs=4))
+        tps = ctx.enter_context(tc.psum_pool(name="tps", bufs=4))
+        accp = ctx.enter_context(tc.psum_pool(name="accp", bufs=4))
+        if MANUAL:
+            ctx.enter_context(tc.manual_schedule())
+
+        taps = (w_now, w_back1, w_back2)
+        first_head = (0, 3, 5)
+
+        def xsrc(n, a):
+            return x[n].rearrange("(m a) k -> m a k", a=4)[:, a, :]
+
+        def wsrc(h, j):
+            return taps[j][h - first_head[j]]
+
+        units = {}
+        for n in range(B):
+            for ap in range(2):
+                units["x%d%d" % (n, ap)] = ("x", [xsrc(n, 2 * ap), xsrc(n, 2 * ap + 1)])
+        wdefs = {
+            "w0": [(0, 0), (1, 0)],
+            "w1": [(3, 0), (4, 0)],
+            "w2": [(3, 1), (4, 1)],
+            "w3": [(5, 0), (6, 0)],
+            "w4": [(5, 1), (6, 1)],
+            "w5": [(5, 2), (6, 2)],
+            "w6": [(2, 0), (7, 0)],
+            "w7": [(7, 1), (7, 2)],
+        }
+        for name, hj in wdefs.items():
+            units[name] = ("w", [wsrc(h, j) for (h, j) in hj])
+
+        load_order = ["w0", "x00", "x01", "x10", "x11", "w1", "w2", "w3", "w4", "w5", "w6", "w7"]
+
+        ones = const.tile([P, P], BF16, name="ones")
+        nc.vector.memset(ones[:], 1.0)
+        dz = const.tile([P, 512], BF16, name="dz")
+        nc.vector.memset(dz[:], 0.0)
+        warm = const.tile([P, 1], F32, name="warm")
+        warm2 = const.tile([P, 1], F32, name="warm2")
+        nc.vector.memset(warm[:], 0.0)
+        nc.scalar.activation(out=warm2[:], in_=warm[:], func=ACT.Copy, scale=1.0)
+        brow = const.tile([P, H * P], BF16, name="brow")
+        nc.vector.memset(brow[:], 0.0)
+        ident = const.tile([P, P], F32, name="ident")
+        make_identity(nc, ident[:])
+        bias_sb = const.tile([P, H, P], F32, name="bias_sb")
+
+        rawt = {}
+        for name in load_order:
+            t = raw.tile([P, 2, D], BF16, name="raw_" + name)
+            rawt[name] = t
+            for i in range(2):
+                nc.sync.dma_start(out=t[:, i, :], in_=units[name][1][i])
+            if name == "x00":
+                nc.sync.dma_start(out=brow[0:1, :], in_=bias.rearrange("(o h) c -> o (h c)", o=1))
+
+        cod = {}
+        sca = {}
+        for name in load_order:
+            cod[name] = codes.tile([P, 512], I32, name="c_" + name, align_bytes=64)
+            sca[name] = codes.tile([P, 512], U8, name="s_" + name, align_bytes=64)
+        for n in range(B):
+            cod["sh%d" % n] = codes.tile([P, 512], I32, name="c_sh%d" % n, align_bytes=64)
+            sca["sh%d" % n] = codes.tile([P, 512], U8, name="s_sh%d" % n, align_bytes=64)
+            nc.vector.memset(cod["sh%d" % n][:], 0)
+            nc.vector.memset(sca["sh%d" % n][:].bitcast(I32), 0)
+            nc.vector.memset(sca["x%d1" % n][:].bitcast(I32), 0)
+
+        pend_q = []
+        pend_c = []
+
+        def stage_t(name, engines):
+            kind = units[name][0]
+            g_t = grp.tile([P, 2048], BF16, name="g_t", tag="g", align_bytes=64)
+            gw = g_t[:].bitcast(F32)
+            if kind == "x":
+                gv = gw.rearrange("p (i g m u) -> p i g m u", i=2, g=2, u=2)
+            else:
+                gv = gw.rearrange("p (g i m u) -> p i g m u", i=2, g=2, u=2)
+            for i in range(2):
+                words = rawt[name][:, i, :].bitcast(F32)
+                pt = tps.tile([P, 4, P], F32, name="pt", tag="pt")
+                for g in range(2):
+                    for u in range(2):
+                        nc.tensor.transpose(pt[:, 2 * g + u, :], words[:, 256 * g + u : 256 * (g + 1) : 2], ident[:])
+                src = pt[:].rearrange("p (g u) m -> p g m u", u=2)
+                if engines[i] == "S":
+                    nc.scalar.copy(out=gv[:, i], in_=src)
+                else:
+                    nc.vector.tensor_copy(out=gv[:, i], in_=src)
+            flush_q()
+            pend_q.append((name, g_t))
+
+        def flush_q():
+            while pend_q:
+                name, g_t = pend_q.pop(0)
+                nc.vector.quantize_mx(out=cod[name][:].bitcast(FP8X4), scales=sca[name][:], in_=g_t[:])
+                if name in ("x01", "x11"):
+                    sh = "sh" + name[1]
+                    nc.vector.tensor_copy(
+                        out=cod[sh][:].rearrange("p (b m) -> p b m", b=4)[:, :, 1:P],
+                        in_=cod[name][:].rearrange("p (b m) -> p b m", b=4)[:, :, 0 : P - 1],
+                    )
+                    nc.vector.tensor_copy(
+                        out=sca[sh][:].rearrange("p (b m) -> p b m", b=4)[:, :, 1:P],
+                        in_=sca[name][:].rearrange("p (b m) -> p b m", b=4)[:, :, 0 : P - 1],
+                    )
+
+        def flush_c():
+            while pend_c:
+                pend_c.pop(0)()
+
+        def lhs(n, a, j, g):
+            s = a - j
+            if s >= 0:
+                name = "x%d%d" % (n, s // 2)
+                off = ((s % 2) * 2 + g) * P
+            else:
+                name = "sh%d" % n
+                off = ((s + 2) * 2 + g) * P
+            return cod[name][:, off : off + P].bitcast(FP8X4), sca[name][:, off : off + P]
+
+        def mm_group(out, n, a, wl, width):
+            passes = [(j, g) for j in range(len(wl)) for g in range(2)]
+            for idx, (j, g) in enumerate(passes):
+                lc, ls = lhs(n, a, j, g)
+                wn, wo = wl[j]
+                c0 = 256 * g + wo
+                nc.tensor.matmul_mx(
+                    out=out,
+                    lhsT=lc,
+                    lhsT_scale=ls,
+                    rhs=cod[wn][:, c0 : c0 + width].bitcast(FP8X4),
+                    rhs_scale=sca[wn][:, c0 : c0 + width],
+                    start=(idx == 0),
+                    stop=(idx == len(passes) - 1),
+                )
+
+        def finish(o_flat, n, hsl, nh):
+            def run():
+                f8 = f8p.tile([P, nh * 512], FP8, name="f8", tag="f8")
+                nc.scalar.activation(out=f8[:], in_=o_flat, func=ACT.Copy, scale=Y_SCALE, saturate=False)
+                nc.sync.dma_start(
+                    out=out_0[n, hsl].rearrange("h (m a) c -> m h (a c)", a=4),
+                    in_=o_flat.rearrange("p (h x) -> p h x", h=nh),
+                )
+                nc.sync.dma_start(
+                    out=out_1[n, hsl].rearrange("h (m a) c -> m h (a c)", a=4),
+                    in_=f8[:].bitcast(U8).rearrange("p (h x) -> p h x", h=nh),
+                )
+            return run
+
+        otiles = {}
+
+        def stage_pair(h0, wnames, n, aps):
+            flush_q()
+            if (h0, n) not in otiles:
+                otiles[(h0, n)] = outp.tile([P, 2, 4, P], F32, name="o", tag="o")
+            o = otiles[(h0, n)]
+            for ap in aps:
+                acc = accp.tile([P, 2, 256], F32, name="acc", tag="acc")
+                for ai in range(2):
+                    mm_group(acc[:, ai, :], n, 2 * ap + ai, [(wn, 0) for wn in wnames], 256)
+                nc.vector.tensor_tensor(
+                    out=o[:, :, 2 * ap : 2 * ap + 2, :],
+                    in0=acc[:].rearrange("p a (h c) -> p h a c", h=2),
+                    in1=bias_sb[:, h0 : h0 + 2, :].unsqueeze(2).to_broadcast([P, 2, 2, P]),
+                    op=ALU.add,
+                )
+            flush_c()
+            if aps[-1] == 1:
+                pend_c.append(finish(o[:].rearrange("p h a c -> p (h a c)"), n, slice(h0, h0 + 2), 2))
+
+        def stage_dummy(count):
+            dps = accp.tile([P, 512], F32, name="acc", tag="acc")
+            for i in range(count):
+                nc.tensor.matmul(out=dps[:], lhsT=ones[:], rhs=dz[:], start=True, stop=True)
+
+        def stage_single(h, wl, n):
+            flush_q()
+            o = outp.tile([P, 4, P], F32, name="o", tag="o")
+            acc = accp.tile([P, 4, P], F32, name="acc", tag="acc")
+            for a in range(4):
+                mm_group(acc[:, a, :], n, a, wl, P)
+            nc.vector.tensor_tensor(
+                out=o[:],
+                in0=acc[:],
+                in1=bias_sb[:, h, :].unsqueeze(1).to_broadcast([P, 4, P]),
+                op=ALU.add,
+            )
+            flush_c()
+            pend_c.append(finish(o[:].rearrange("p a c -> p (a c)"), n, slice(h, h + 1), 1))
+
+        def stage_bias():
+            for half in range(2):
+                bp = accp.tile([P, 512], F32, name="acc", tag="acc")
+                nc.tensor.matmul(out=bp[:], lhsT=ones[:], rhs=brow[:, 512 * half : 512 * (half + 1)], start=True, stop=True)
+                nc.vector.tensor_copy(
+                    out=bias_sb[:, 4 * half : 4 * half + 4, :].rearrange("p h c -> p (h c)"), in_=bp[:]
+                )
+
+        stage_dummy(5)
+        stage_t("w0", "SV")
+        stage_t("x00", "SV")
+        stage_bias()
+        stage_t("x01", "SS")
+        stage_pair(0, ["w0"], 0, [0])
+        stage_t("x10", "SS")
+        stage_pair(0, ["w0"], 0, [1])
+        stage_t("x11", "SS")
+        stage_pair(0, ["w0"], 1, [0])
+        stage_t("w1", "SS")
+        stage_pair(0, ["w0"], 1, [1])
+        stage_t("w2", "SS")
+        stage_t("w3", "SS")
+        stage_pair(3, ["w1", "w2"], 0, [0, 1])
+        stage_t("w4", "SS")
+        stage_t("w5", "SS")
+        stage_pair(3, ["w1", "w2"], 1, [0, 1])
+        stage_t("w6", "SS")
+        stage_t("w7", "SS")
+        stage_pair(5, ["w3", "w4", "w5"], 0, [0, 1])
+        stage_pair(5, ["w3", "w4", "w5"], 1, [0, 1])
+        stage_single(7, [("w6", P), ("w7", 0), ("w7", P)], 0)
+        stage_single(7, [("w6", P), ("w7", 0), ("w7", P)], 1)
+        stage_single(2, [("w6", 0)], 0)
+        stage_single(2, [("w6", 0)], 1)
+        flush_c()

@@ -16,7 +16,6 @@ ALU = mybir.AluOpType
 ACT = mybir.ActivationFunctionType
 
 Y_SCALE = 140.0
-MANUAL = True
 
 
 def tile_multiheadhomogeneousattention_pa_kernel(tc, x, w_now, w_back1, w_back2, bias, out_0, out_1):
@@ -30,47 +29,42 @@ def tile_multiheadhomogeneousattention_pa_kernel(tc, x, w_now, w_back1, w_back2,
         f8p = ctx.enter_context(tc.tile_pool(name="f8p", bufs=4))
         tps = ctx.enter_context(tc.psum_pool(name="tps", bufs=4))
         accp = ctx.enter_context(tc.psum_pool(name="accp", bufs=4))
-        if MANUAL:
-            ctx.enter_context(tc.manual_schedule())
+        ctx.enter_context(tc.manual_schedule())
 
-        taps = (w_now, w_back1, w_back2)
-        first_head = (0, 3, 5)
+        def xview(n, ap):
+            return x[n].rearrange("(m a) k -> m a k", a=4)[:, 2 * ap : 2 * ap + 2, :]
 
-        def xsrc(n, a):
-            return x[n].rearrange("(m a) k -> m a k", a=4)[:, a, :]
-
-        def wsrc(h, j):
-            return taps[j][h - first_head[j]]
-
-        units = {}
-        for n in range(B):
-            for ap in range(2):
-                units["x%d%d" % (n, ap)] = ("x", [xsrc(n, 2 * ap), xsrc(n, 2 * ap + 1)])
-        wdefs = {
-            "w0": [(0, 0), (1, 0)],
-            "w1": [(3, 0), (4, 0)],
-            "w2": [(3, 1), (4, 1)],
-            "w3": [(5, 0), (6, 0)],
-            "w4": [(5, 1), (6, 1)],
-            "w5": [(5, 2), (6, 2)],
-            "w6": [(2, 0), (7, 0)],
-            "w7": [(7, 1), (7, 2)],
+        srcs = {
+            "x00": [(xview(0, 0), 0, 2)],
+            "x01": [(xview(0, 1), 0, 2)],
+            "x10": [(xview(1, 0), 0, 2)],
+            "x11": [(xview(1, 1), 0, 2)],
+            "w0": [(w_now[0:2].rearrange("h c k -> c h k"), 0, 2)],
+            "w1": [(w_now[3:5].rearrange("h c k -> c h k"), 0, 2)],
+            "w2": [(w_back1[0:2].rearrange("h c k -> c h k"), 0, 2)],
+            "w3": [(w_now[5:7].rearrange("h c k -> c h k"), 0, 2)],
+            "w4": [(w_back1[2:4].rearrange("h c k -> c h k"), 0, 2)],
+            "w5": [(w_back2[0:2].rearrange("h c k -> c h k"), 0, 2)],
+            "w6": [(w_now[2:8:5].rearrange("h c k -> c h k"), 0, 2)],
+            "w7": [
+                (w_back1[4:5].rearrange("h c k -> c h k"), 0, 1),
+                (w_back2[2:3].rearrange("h c k -> c h k"), 1, 1),
+            ],
         }
-        for name, hj in wdefs.items():
-            units[name] = ("w", [wsrc(h, j) for (h, j) in hj])
-
-        load_order = ["w0", "x00", "x01", "x10", "x11", "w1", "w2", "w3", "w4", "w5", "w6", "w7"]
+        load_order = ["w0", "x00", "x01", "w1", "w2", "x10", "x11", "w3", "w4", "w5", "w6", "w7"]
+        split = {"w0": 4, "x00": 4, "x01": 2, "w1": 2, "w2": 2}
 
         ones = const.tile([P, P], BF16, name="ones")
-        nc.vector.memset(ones[:], 1.0)
+        nc.gpsimd.memset(ones[:], 1.0)
         dz = const.tile([P, 512], BF16, name="dz")
-        nc.vector.memset(dz[:], 0.0)
+        nc.gpsimd.memset(dz[:], 0.0)
+        brow = const.tile([P, H * P], BF16, name="brow")
+        nc.vector.memset(brow[:], 0.0)
+        nc.scalar.dma_start(out=brow[0:1, :], in_=bias.rearrange("(o h) c -> o (h c)", o=1))
         warm = const.tile([P, 1], F32, name="warm")
         warm2 = const.tile([P, 1], F32, name="warm2")
         nc.vector.memset(warm[:], 0.0)
         nc.scalar.activation(out=warm2[:], in_=warm[:], func=ACT.Copy, scale=1.0)
-        brow = const.tile([P, H * P], BF16, name="brow")
-        nc.vector.memset(brow[:], 0.0)
         ident = const.tile([P, P], F32, name="ident")
         make_identity(nc, ident[:])
         bias_sb = const.tile([P, H, P], F32, name="bias_sb")
@@ -79,10 +73,15 @@ def tile_multiheadhomogeneousattention_pa_kernel(tc, x, w_now, w_back1, w_back2,
         for name in load_order:
             t = raw.tile([P, 2, D], BF16, name="raw_" + name)
             rawt[name] = t
-            for i in range(2):
-                nc.sync.dma_start(out=t[:, i, :], in_=units[name][1][i])
-            if name == "x00":
-                nc.sync.dma_start(out=brow[0:1, :], in_=bias.rearrange("(o h) c -> o (h c)", o=1))
+            parts = split.get(name, 1)
+            for (view, i0, ni) in srcs[name]:
+                if parts == 1:
+                    nc.sync.dma_start(out=t[:, i0 : i0 + ni, :], in_=view)
+                else:
+                    for i in range(ni):
+                        for g in range(parts // 2):
+                            w = D // (parts // 2)
+                            nc.sync.dma_start(out=t[:, i0 + i, g * w : (g + 1) * w], in_=view[:, i, g * w : (g + 1) * w])
 
         cod = {}
         sca = {}
@@ -98,28 +97,6 @@ def tile_multiheadhomogeneousattention_pa_kernel(tc, x, w_now, w_back1, w_back2,
 
         pend_q = []
         pend_c = []
-
-        def stage_t(name, engines):
-            kind = units[name][0]
-            g_t = grp.tile([P, 2048], BF16, name="g_t", tag="g", align_bytes=64)
-            gw = g_t[:].bitcast(F32)
-            if kind == "x":
-                gv = gw.rearrange("p (i g m u) -> p i g m u", i=2, g=2, u=2)
-            else:
-                gv = gw.rearrange("p (g i m u) -> p i g m u", i=2, g=2, u=2)
-            for i in range(2):
-                words = rawt[name][:, i, :].bitcast(F32)
-                pt = tps.tile([P, 4, P], F32, name="pt", tag="pt")
-                for g in range(2):
-                    for u in range(2):
-                        nc.tensor.transpose(pt[:, 2 * g + u, :], words[:, 256 * g + u : 256 * (g + 1) : 2], ident[:])
-                src = pt[:].rearrange("p (g u) m -> p g m u", u=2)
-                if engines[i] == "S":
-                    nc.scalar.copy(out=gv[:, i], in_=src)
-                else:
-                    nc.vector.tensor_copy(out=gv[:, i], in_=src)
-            flush_q()
-            pend_q.append((name, g_t))
 
         def flush_q():
             while pend_q:
@@ -139,6 +116,23 @@ def tile_multiheadhomogeneousattention_pa_kernel(tc, x, w_now, w_back1, w_back2,
         def flush_c():
             while pend_c:
                 pend_c.pop(0)()
+
+        def stage_t(name):
+            g_t = grp.tile([P, 2048], BF16, name="g_t", tag="g", align_bytes=64)
+            gw = g_t[:].bitcast(F32)
+            if name[0] == "x":
+                gv = gw.rearrange("p (i g m u) -> p i g m u", i=2, g=2, u=2)
+            else:
+                gv = gw.rearrange("p (g i m u) -> p i g m u", i=2, g=2, u=2)
+            for i in range(2):
+                words = rawt[name][:, i, :].bitcast(F32)
+                pt = tps.tile([P, 4, P], F32, name="pt", tag="pt")
+                for g in range(2):
+                    for u in range(2):
+                        nc.tensor.transpose(pt[:, 2 * g + u, :], words[:, 256 * g + u : 256 * (g + 1) : 2], ident[:])
+                nc.scalar.copy(out=gv[:, i], in_=pt[:].rearrange("p (g u) m -> p g m u", u=2))
+            flush_q()
+            pend_q.append((name, g_t))
 
         def lhs(n, a, j, g):
             s = a - j
@@ -166,23 +160,27 @@ def tile_multiheadhomogeneousattention_pa_kernel(tc, x, w_now, w_back1, w_back2,
                     stop=(idx == len(passes) - 1),
                 )
 
-        def finish(o_flat, n, hsl, nh):
+        def finish(o_view, dst0, dst1, engine):
+            nh, cols = o_view.shape[1], o_view.shape[2]
+
             def run():
-                f8 = f8p.tile([P, nh * 512], FP8, name="f8", tag="f8")
-                nc.scalar.activation(out=f8[:], in_=o_flat, func=ACT.Copy, scale=Y_SCALE, saturate=False)
-                nc.sync.dma_start(
-                    out=out_0[n, hsl].rearrange("h (m a) c -> m h (a c)", a=4),
-                    in_=o_flat.rearrange("p (h x) -> p h x", h=nh),
-                )
-                nc.sync.dma_start(
-                    out=out_1[n, hsl].rearrange("h (m a) c -> m h (a c)", a=4),
-                    in_=f8[:].bitcast(U8).rearrange("p (h x) -> p h x", h=nh),
-                )
+                f8 = f8p.tile([P, nh * cols], FP8, name="f8", tag="f8")
+                nc.sync.dma_start(out=dst0, in_=o_view)
+                flat = o_view.rearrange("p h x -> p (h x)")
+                if engine == "S":
+                    nc.scalar.activation(out=f8[:], in_=flat, func=ACT.Copy, scale=Y_SCALE, saturate=False)
+                else:
+                    nc.vector.tensor_scalar(out=f8[:], in0=flat, scalar1=Y_SCALE, scalar2=None, op0=ALU.mult, saturate=False)
+                nc.sync.dma_start(out=dst1, in_=f8[:].bitcast(U8).rearrange("p (h x) -> p h x", h=nh))
+
             return run
+
+        def dview(dst, n, hsl, a0, na):
+            return dst[n, hsl].rearrange("h (m a) c -> m h a c", a=4)[:, :, a0 : a0 + na, :].rearrange("m h a c -> m h (a c)")
 
         otiles = {}
 
-        def stage_pair(h0, wnames, n, aps):
+        def stage_pair(h0, wnames, n, aps, engine):
             flush_q()
             if (h0, n) not in otiles:
                 otiles[(h0, n)] = outp.tile([P, 2, 4, P], F32, name="o", tag="o")
@@ -199,60 +197,71 @@ def tile_multiheadhomogeneousattention_pa_kernel(tc, x, w_now, w_back1, w_back2,
                 )
             flush_c()
             if aps[-1] == 1:
-                pend_c.append(finish(o[:].rearrange("p h a c -> p (h a c)"), n, slice(h0, h0 + 2), 2))
+                hsl = slice(h0, h0 + 2)
+                pend_c.append(
+                    finish(o[:].rearrange("p h a c -> p h (a c)"), dview(out_0, n, hsl, 0, 4), dview(out_1, n, hsl, 0, 4), engine)
+                )
+
+        def stage_single(h, wl, n, pieces, engine):
+            flush_q()
+            o = outp.tile([P, 4, P], F32, name="o", tag="o")
+            na = 4 // pieces
+            hsl = slice(h, h + 1)
+            for q in range(pieces):
+                acc = accp.tile([P, na, P], F32, name="acc", tag="acc")
+                for ai in range(na):
+                    mm_group(acc[:, ai, :], n, q * na + ai, wl, P)
+                nc.vector.tensor_tensor(
+                    out=o[:, q * na : (q + 1) * na, :],
+                    in0=acc[:],
+                    in1=bias_sb[:, h, :].unsqueeze(1).to_broadcast([P, na, P]),
+                    op=ALU.add,
+                )
+                flush_c()
+                pend_c.append(
+                    finish(
+                        o[:, q * na : (q + 1) * na, :].rearrange("p a c -> p (a c)").unsqueeze(1),
+                        dview(out_0, n, hsl, q * na, na),
+                        dview(out_1, n, hsl, q * na, na),
+                        engine[q],
+                    )
+                )
+
+        def stage_bias(half):
+            bp = accp.tile([P, 512], F32, name="acc", tag="acc")
+            nc.tensor.matmul(out=bp[:], lhsT=ones[:], rhs=brow[:, 512 * half : 512 * (half + 1)], start=True, stop=True)
+            nc.scalar.copy(out=bias_sb[:, 4 * half : 4 * half + 4, :].rearrange("p h c -> p (h c)"), in_=bp[:])
 
         def stage_dummy(count):
             dps = accp.tile([P, 512], F32, name="acc", tag="acc")
             for i in range(count):
-                nc.tensor.matmul(out=dps[:], lhsT=ones[:], rhs=dz[:], start=True, stop=True)
+                nc.tensor.matmul(out=dps[:], lhsT=ones[:], rhs=dz[:], start=(i == 0), stop=(i == count - 1))
 
-        def stage_single(h, wl, n):
-            flush_q()
-            o = outp.tile([P, 4, P], F32, name="o", tag="o")
-            acc = accp.tile([P, 4, P], F32, name="acc", tag="acc")
-            for a in range(4):
-                mm_group(acc[:, a, :], n, a, wl, P)
-            nc.vector.tensor_tensor(
-                out=o[:],
-                in0=acc[:],
-                in1=bias_sb[:, h, :].unsqueeze(1).to_broadcast([P, 4, P]),
-                op=ALU.add,
-            )
-            flush_c()
-            pend_c.append(finish(o[:].rearrange("p a c -> p (a c)"), n, slice(h, h + 1), 1))
-
-        def stage_bias():
-            for half in range(2):
-                bp = accp.tile([P, 512], F32, name="acc", tag="acc")
-                nc.tensor.matmul(out=bp[:], lhsT=ones[:], rhs=brow[:, 512 * half : 512 * (half + 1)], start=True, stop=True)
-                nc.vector.tensor_copy(
-                    out=bias_sb[:, 4 * half : 4 * half + 4, :].rearrange("p h c -> p (h c)"), in_=bp[:]
-                )
-
-        stage_dummy(5)
-        stage_t("w0", "SV")
-        stage_t("x00", "SV")
-        stage_bias()
-        stage_t("x01", "SS")
-        stage_pair(0, ["w0"], 0, [0])
-        stage_t("x10", "SS")
-        stage_pair(0, ["w0"], 0, [1])
-        stage_t("x11", "SS")
-        stage_pair(0, ["w0"], 1, [0])
-        stage_t("w1", "SS")
-        stage_pair(0, ["w0"], 1, [1])
-        stage_t("w2", "SS")
-        stage_t("w3", "SS")
-        stage_pair(3, ["w1", "w2"], 0, [0, 1])
-        stage_t("w4", "SS")
-        stage_t("w5", "SS")
-        stage_pair(3, ["w1", "w2"], 1, [0, 1])
-        stage_t("w6", "SS")
-        stage_t("w7", "SS")
-        stage_pair(5, ["w3", "w4", "w5"], 0, [0, 1])
-        stage_pair(5, ["w3", "w4", "w5"], 1, [0, 1])
-        stage_single(7, [("w6", P), ("w7", 0), ("w7", P)], 0)
-        stage_single(7, [("w6", P), ("w7", 0), ("w7", P)], 1)
-        stage_single(2, [("w6", 0)], 0)
-        stage_single(2, [("w6", 0)], 1)
+        h7 = [("w6", P), ("w7", 0), ("w7", P)]
+        stage_dummy(4)
+        stage_t("w0")
+        stage_bias(0)
+        stage_t("x00")
+        stage_bias(1)
+        stage_t("x01")
+        stage_pair(0, ["w0"], 0, [0], "S")
+        stage_t("w1")
+        stage_t("w2")
+        stage_pair(0, ["w0"], 0, [1], "S")
+        stage_t("x10")
+        stage_pair(3, ["w1", "w2"], 0, [0, 1], "S")
+        stage_t("x11")
+        stage_t("w3")
+        stage_pair(0, ["w0"], 1, [0, 1], "S")
+        stage_t("w4")
+        stage_t("w5")
+        stage_pair(3, ["w1", "w2"], 1, [0, 1], "S")
+        stage_t("w6")
+        stage_t("w7")
+        stage_pair(5, ["w3", "w4", "w5"], 0, [0, 1], "S")
+        stage_pair(5, ["w3", "w4", "w5"], 1, [0, 1], "S")
+        stage_single(2, [("w6", 0)], 0, 1, "S")
+        stage_single(2, [("w6", 0)], 1, 1, "S")
+        stage_single(7, h7, 0, 1, "S")
+        stage_single(7, h7, 1, 2, "SV")
         flush_c()

@@ -17,6 +17,17 @@ ACT = mybir.ActivationFunctionType
 
 Y_SCALE = 140.0
 
+LOAD_ORDER = ["x00","x01","w3","w4","w5","x10","x11","w0","w1","w2","w6","w7"]
+SPLIT = {"x00":4,"x01":4,"w3":2,"w4":2,"w5":2}
+
+PLAN = """
+D4 T:x00:d Q:x00 T:x01:d Q:x01 T:w3:d Q:w3 S:0 T:w4:d Q:w4 T:w5:d B0 B1 Q:w5 T:x10:d Q:x10 T:x11:d R:w0 Q:x11 R:w1 S:1
+M:C01 M:C00 A:C01 T:w0 T:w1 A:C00 F:C0 R:w2 R:w6
+M:C10 Q:w0 M:C11 A:C10 Q:w1 T:w2 T:w6 A:C11 F:C1 R:w7
+M:A00 M:A01 A:A00 M:A10 A:A01 F:A0 M:A11 A:A10 Q:w2 T:w7 A:A11 F:A1 Q:w6
+M:B00 M:B01 A:B00 Q:w7 M:B10 A:B01 F:B0 M:B11 A:B10 M:D0 A:B11 F:B1 M:D1 A:D0 F:D0 M:E0 A:D1 F:D1 M:E1a A:E0 F:E0 M:E1b A:E1a F:E1a A:E1b F:E1b:V
+"""
+
 
 def tile_multiheadhomogeneousattention_pa_kernel(tc, x, w_now, w_back1, w_back2, bias, out_0, out_1):
     nc = tc.nc
@@ -24,9 +35,10 @@ def tile_multiheadhomogeneousattention_pa_kernel(tc, x, w_now, w_back1, w_back2,
         const = ctx.enter_context(tc.tile_pool(name="const", bufs=1))
         raw = ctx.enter_context(tc.tile_pool(name="raw", bufs=1))
         codes = ctx.enter_context(tc.tile_pool(name="codes", bufs=1))
-        grp = ctx.enter_context(tc.tile_pool(name="grp", bufs=3))
-        outp = ctx.enter_context(tc.tile_pool(name="outp", bufs=4))
-        f8p = ctx.enter_context(tc.tile_pool(name="f8p", bufs=4))
+        grp = ctx.enter_context(tc.tile_pool(name="grp", bufs=4))
+        reo = ctx.enter_context(tc.tile_pool(name="reo", bufs=4))
+        outp = ctx.enter_context(tc.tile_pool(name="outp", bufs=1))
+        f8p = ctx.enter_context(tc.tile_pool(name="f8p", bufs=6))
         tps = ctx.enter_context(tc.psum_pool(name="tps", bufs=4))
         accp = ctx.enter_context(tc.psum_pool(name="accp", bufs=4))
         ctx.enter_context(tc.manual_schedule())
@@ -51,8 +63,6 @@ def tile_multiheadhomogeneousattention_pa_kernel(tc, x, w_now, w_back1, w_back2,
                 (w_back2[2:3].rearrange("h c k -> c h k"), 1, 1),
             ],
         }
-        load_order = ["w0", "x00", "x01", "w1", "w2", "x10", "x11", "w3", "w4", "w5", "w6", "w7"]
-        split = {"w0": 4, "x00": 4, "x01": 2, "w1": 2, "w2": 2}
 
         ones = const.tile([P, P], BF16, name="ones")
         nc.gpsimd.memset(ones[:], 1.0)
@@ -70,10 +80,10 @@ def tile_multiheadhomogeneousattention_pa_kernel(tc, x, w_now, w_back1, w_back2,
         bias_sb = const.tile([P, H, P], F32, name="bias_sb")
 
         rawt = {}
-        for name in load_order:
+        for name in LOAD_ORDER:
             t = raw.tile([P, 2, D], BF16, name="raw_" + name)
             rawt[name] = t
-            parts = split.get(name, 1)
+            parts = SPLIT.get(name, 1)
             for (view, i0, ni) in srcs[name]:
                 if parts == 1:
                     nc.sync.dma_start(out=t[:, i0 : i0 + ni, :], in_=view)
@@ -85,7 +95,7 @@ def tile_multiheadhomogeneousattention_pa_kernel(tc, x, w_now, w_back1, w_back2,
 
         cod = {}
         sca = {}
-        for name in load_order:
+        for name in LOAD_ORDER:
             cod[name] = codes.tile([P, 512], I32, name="c_" + name, align_bytes=64)
             sca[name] = codes.tile([P, 512], U8, name="s_" + name, align_bytes=64)
         for n in range(B):
@@ -95,44 +105,57 @@ def tile_multiheadhomogeneousattention_pa_kernel(tc, x, w_now, w_back1, w_back2,
             nc.vector.memset(sca["sh%d" % n][:].bitcast(I32), 0)
             nc.vector.memset(sca["x%d1" % n][:].bitcast(I32), 0)
 
-        pend_q = []
-        pend_c = []
+        reot = {}
+        grpt = {}
 
-        def flush_q():
-            while pend_q:
-                name, g_t = pend_q.pop(0)
-                nc.vector.quantize_mx(out=cod[name][:].bitcast(FP8X4), scales=sca[name][:], in_=g_t[:])
-                if name in ("x01", "x11"):
-                    sh = "sh" + name[1]
-                    nc.vector.tensor_copy(
-                        out=cod[sh][:].rearrange("p (b m) -> p b m", b=4)[:, :, 1:P],
-                        in_=cod[name][:].rearrange("p (b m) -> p b m", b=4)[:, :, 0 : P - 1],
-                    )
-                    nc.vector.tensor_copy(
-                        out=sca[sh][:].rearrange("p (b m) -> p b m", b=4)[:, :, 1:P],
-                        in_=sca[name][:].rearrange("p (b m) -> p b m", b=4)[:, :, 0 : P - 1],
-                    )
+        def stage_r(name, pieces=1):
+            r_t = reo.tile([P, 2, 512], F32, name="r_t", tag="r")
+            reot[name] = r_t
+            words = rawt[name][:].rearrange("p i k -> p (i k)").bitcast(F32)
+            w = 512 // pieces
+            for q in range(pieces):
+                nc.vector.tensor_copy(
+                    out=r_t[:, :, q * w : (q + 1) * w],
+                    in_=words[:, 2 * q * w : 2 * (q + 1) * w].rearrange("p (m u) -> p u m", u=2),
+                )
 
-        def flush_c():
-            while pend_c:
-                pend_c.pop(0)()
+        def stage_q(name):
+            nc.vector.quantize_mx(out=cod[name][:].bitcast(FP8X4), scales=sca[name][:], in_=grpt[name][:])
 
-        def stage_t(name):
+        def stage_s(n):
+            if True:
+                sh = "sh%d" % n
+                name = "x%d1" % n
+                nc.vector.tensor_copy(
+                    out=cod[sh][:].rearrange("p (b m) -> p b m", b=4)[:, :, 1:P],
+                    in_=cod[name][:].rearrange("p (b m) -> p b m", b=4)[:, :, 0 : P - 1],
+                )
+                nc.vector.tensor_copy(
+                    out=sca[sh][:].rearrange("p (b m) -> p b m", b=4)[:, :, 1:P],
+                    in_=sca[name][:].rearrange("p (b m) -> p b m", b=4)[:, :, 0 : P - 1],
+                )
+
+        def stage_t(name, direct, engines):
             g_t = grp.tile([P, 2048], BF16, name="g_t", tag="g", align_bytes=64)
+            grpt[name] = g_t
             gw = g_t[:].bitcast(F32)
             if name[0] == "x":
                 gv = gw.rearrange("p (i g m u) -> p i g m u", i=2, g=2, u=2)
             else:
                 gv = gw.rearrange("p (g i m u) -> p i g m u", i=2, g=2, u=2)
             for i in range(2):
-                words = rawt[name][:, i, :].bitcast(F32)
                 pt = tps.tile([P, 4, P], F32, name="pt", tag="pt")
                 for g in range(2):
                     for u in range(2):
-                        nc.tensor.transpose(pt[:, 2 * g + u, :], words[:, 256 * g + u : 256 * (g + 1) : 2], ident[:])
-                nc.scalar.copy(out=gv[:, i], in_=pt[:].rearrange("p (g u) m -> p g m u", u=2))
-            flush_q()
-            pend_q.append((name, g_t))
+                        if direct:
+                            src = rawt[name][:, i, :].bitcast(F32)[:, 256 * g + u : 256 * (g + 1) : 2]
+                        else:
+                            src = reot[name][:, u, (2 * i + g) * P : (2 * i + g + 1) * P]
+                        nc.tensor.transpose(pt[:, 2 * g + u, :], src, ident[:])
+                if engines[i] == "S":
+                    nc.scalar.copy(out=gv[:, i], in_=pt[:].rearrange("p (g u) m -> p g m u", u=2))
+                else:
+                    nc.vector.tensor_copy(out=gv[:, i], in_=pt[:].rearrange("p (g u) m -> p g m u", u=2))
 
         def lhs(n, a, j, g):
             s = a - j
@@ -160,72 +183,64 @@ def tile_multiheadhomogeneousattention_pa_kernel(tc, x, w_now, w_back1, w_back2,
                     stop=(idx == len(passes) - 1),
                 )
 
-        def finish(o_view, dst0, dst1, engine):
-            nh, cols = o_view.shape[1], o_view.shape[2]
-
-            def run():
-                f8 = f8p.tile([P, nh * cols], FP8, name="f8", tag="f8")
-                nc.sync.dma_start(out=dst0, in_=o_view)
-                flat = o_view.rearrange("p h x -> p (h x)")
-                if engine == "S":
-                    nc.scalar.activation(out=f8[:], in_=flat, func=ACT.Copy, scale=Y_SCALE, saturate=False)
-                else:
-                    nc.vector.tensor_scalar(out=f8[:], in0=flat, scalar1=Y_SCALE, scalar2=None, op0=ALU.mult, saturate=False)
-                nc.sync.dma_start(out=dst1, in_=f8[:].bitcast(U8).rearrange("p (h x) -> p h x", h=nh))
-
-            return run
-
         def dview(dst, n, hsl, a0, na):
             return dst[n, hsl].rearrange("h (m a) c -> m h a c", a=4)[:, :, a0 : a0 + na, :].rearrange("m h a c -> m h (a c)")
 
-        otiles = {}
+        KIND = {
+            "A": (0, 2, [("w0", 0)]),
+            "B": (3, 2, [("w1", 0), ("w2", 0)]),
+            "C": (5, 2, [("w3", 0), ("w4", 0), ("w5", 0)]),
+            "D": (2, 1, [("w6", 0)]),
+            "E": (7, 1, [("w6", P), ("w7", 0), ("w7", P)]),
+        }
+        otile = {}
+        accs = {}
 
-        def stage_pair(h0, wnames, n, aps, engine):
-            flush_q()
-            if (h0, n) not in otiles:
-                otiles[(h0, n)] = outp.tile([P, 2, 4, P], F32, name="o", tag="o")
-            o = otiles[(h0, n)]
-            for ap in aps:
-                acc = accp.tile([P, 2, 256], F32, name="acc", tag="acc")
-                for ai in range(2):
-                    mm_group(acc[:, ai, :], n, 2 * ap + ai, [(wn, 0) for wn in wnames], 256)
-                nc.vector.tensor_tensor(
-                    out=o[:, :, 2 * ap : 2 * ap + 2, :],
-                    in0=acc[:].rearrange("p a (h c) -> p h a c", h=2),
-                    in1=bias_sb[:, h0 : h0 + 2, :].unsqueeze(2).to_broadcast([P, 2, 2, P]),
-                    op=ALU.add,
-                )
-            flush_c()
-            if aps[-1] == 1:
-                hsl = slice(h0, h0 + 2)
-                pend_c.append(
-                    finish(o[:].rearrange("p h a c -> p h (a c)"), dview(out_0, n, hsl, 0, 4), dview(out_1, n, hsl, 0, 4), engine)
-                )
+        def block_range(b):
+            k = b[0]
+            if KIND[k][1] == 2:
+                return 2 * int(b[2]), 2
+            if len(b) == 2:
+                return 0, 4
+            return {"a": (0, 2), "b": (2, 2), "c": (2, 1), "d": (3, 1)}[b[2]]
 
-        def stage_single(h, wl, n, pieces, engine):
-            flush_q()
-            o = outp.tile([P, 4, P], F32, name="o", tag="o")
-            na = 4 // pieces
-            hsl = slice(h, h + 1)
-            for q in range(pieces):
-                acc = accp.tile([P, na, P], F32, name="acc", tag="acc")
-                for ai in range(na):
-                    mm_group(acc[:, ai, :], n, q * na + ai, wl, P)
-                nc.vector.tensor_tensor(
-                    out=o[:, q * na : (q + 1) * na, :],
-                    in0=acc[:],
-                    in1=bias_sb[:, h, :].unsqueeze(1).to_broadcast([P, na, P]),
-                    op=ALU.add,
-                )
-                flush_c()
-                pend_c.append(
-                    finish(
-                        o[:, q * na : (q + 1) * na, :].rearrange("p a c -> p (a c)").unsqueeze(1),
-                        dview(out_0, n, hsl, q * na, na),
-                        dview(out_1, n, hsl, q * na, na),
-                        engine[q],
-                    )
-                )
+        def stage_m(b):
+            h0, nh, wl = KIND[b[0]]
+            n = int(b[1])
+            a0, na = block_range(b)
+            acc = accp.tile([P, na, nh * P], F32, name="acc", tag="acc")
+            accs[b] = acc
+            for ai in range(na):
+                mm_group(acc[:, ai, :], n, a0 + ai, wl, nh * P)
+
+        def stage_a(b):
+            h0, nh, wl = KIND[b[0]]
+            a0, na = block_range(b)
+            key = b[0:2]
+            if key not in otile:
+                otile[key] = outp.tile([P, nh, 4, P], F32, name="o_" + key)
+            o = otile[key]
+            nc.vector.tensor_tensor(
+                out=o[:, :, a0 : a0 + na, :],
+                in0=accs[b][:].rearrange("p a (h c) -> p h a c", h=nh),
+                in1=bias_sb[:, h0 : h0 + nh, :].unsqueeze(2).to_broadcast([P, nh, na, P]),
+                op=ALU.add,
+            )
+
+        def stage_f(b, engine):
+            h0, nh, wl = KIND[b[0]]
+            n = int(b[1])
+            a0, na = (0, 4) if len(b) == 2 else block_range(b)
+            o_view = otile[b[0:2]][:, :, a0 : a0 + na, :].rearrange("p h a c -> p h (a c)")
+            hsl = slice(h0, h0 + nh)
+            f8 = f8p.tile([P, nh * na * P], FP8, name="f8", tag="f8")
+            nc.sync.dma_start(out=dview(out_0, n, hsl, a0, na), in_=o_view)
+            flat = o_view.rearrange("p h x -> p (h x)")
+            if engine == "S":
+                nc.scalar.activation(out=f8[:], in_=flat, func=ACT.Copy, scale=Y_SCALE, saturate=False)
+            else:
+                nc.vector.tensor_scalar(out=f8[:], in0=flat, scalar1=Y_SCALE, scalar2=None, op0=ALU.mult, saturate=False)
+            nc.sync.dma_start(out=dview(out_1, n, hsl, a0, na), in_=f8[:].bitcast(U8).rearrange("p (h x) -> p h x", h=nh))
 
         def stage_bias(half):
             bp = accp.tile([P, 512], F32, name="acc", tag="acc")
@@ -237,31 +252,24 @@ def tile_multiheadhomogeneousattention_pa_kernel(tc, x, w_now, w_back1, w_back2,
             for i in range(count):
                 nc.tensor.matmul(out=dps[:], lhsT=ones[:], rhs=dz[:], start=(i == 0), stop=(i == count - 1))
 
-        h7 = [("w6", P), ("w7", 0), ("w7", P)]
-        stage_dummy(4)
-        stage_t("w0")
-        stage_bias(0)
-        stage_t("x00")
-        stage_bias(1)
-        stage_t("x01")
-        stage_pair(0, ["w0"], 0, [0], "S")
-        stage_t("w1")
-        stage_t("w2")
-        stage_pair(0, ["w0"], 0, [1], "S")
-        stage_t("x10")
-        stage_pair(3, ["w1", "w2"], 0, [0, 1], "S")
-        stage_t("x11")
-        stage_t("w3")
-        stage_pair(0, ["w0"], 1, [0, 1], "S")
-        stage_t("w4")
-        stage_t("w5")
-        stage_pair(3, ["w1", "w2"], 1, [0, 1], "S")
-        stage_t("w6")
-        stage_t("w7")
-        stage_pair(5, ["w3", "w4", "w5"], 0, [0, 1], "S")
-        stage_pair(5, ["w3", "w4", "w5"], 1, [0, 1], "S")
-        stage_single(2, [("w6", 0)], 0, 1, "S")
-        stage_single(2, [("w6", 0)], 1, 1, "S")
-        stage_single(7, h7, 0, 1, "S")
-        stage_single(7, h7, 1, 2, "SV")
-        flush_c()
+        for item in PLAN.split():
+            f = item.split(":")
+            if f[0][0] == "D" and len(f) == 1:
+                stage_dummy(int(f[0][1:]))
+            elif f[0][0] == "B" and len(f) == 1:
+                stage_bias(int(f[0][1:]))
+            elif f[0] == "R":
+                stage_r(f[1], int(f[2]) if len(f) > 2 else 1)
+            elif f[0] == "T":
+                opts = f[2] if len(f) > 2 else ""
+                stage_t(f[1], "d" in opts, "SV" if "v" in opts else "SS")
+            elif f[0] == "Q":
+                stage_q(f[1])
+            elif f[0] == "S":
+                stage_s(int(f[1]))
+            elif f[0] == "M":
+                stage_m(f[1])
+            elif f[0] == "A":
+                stage_a(f[1])
+            elif f[0] == "F":
+                stage_f(f[1], f[2] if len(f) > 2 else "S")

@@ -21,7 +21,7 @@ LOAD_ORDER = ["x00","x01","w3","w4","w5","x10","x11","w0","w1","w2","w6","w7"]
 SPLIT = {"x00":4,"x01":4,"w3":2,"w4":2,"w5":2}
 
 PLAN = """
-D4 T:x00:d Q:x00 T:x01:d Q:x01 T:w3:d Q:w3 S:0 T:w4:d Q:w4 T:w5:d B0 B1 Q:w5 T:x10:d Q:x10 T:x11:d R:w0 Q:x11 R:w1 S:1
+T:x00:d Q:x00 T:x01:d Q:x01 T:w3:d Q:w3 S:0 T:w4:d Q:w4 T:w5:d B0 B1 Q:w5 T:x10:d Q:x10 T:x11:d R:w0 Q:x11 R:w1 S:1
 M:C01 M:C00 A:C01 T:w0 T:w1 A:C00 F:C0 R:w2 R:w6
 M:C10 Q:w0 M:C11 A:C10 Q:w1 T:w2 T:w6 A:C11 F:C1 R:w7
 M:A00 M:A01 A:A00 M:A10 A:A01 F:A0 M:A11 A:A10 Q:w2 T:w7 A:A11 F:A1 Q:w6
@@ -66,8 +66,6 @@ def tile_multiheadhomogeneousattention_pa_kernel(tc, x, w_now, w_back1, w_back2,
 
         ones = const.tile([P, P], BF16, name="ones")
         nc.gpsimd.memset(ones[:], 1.0)
-        dz = const.tile([P, 512], BF16, name="dz")
-        nc.gpsimd.memset(dz[:], 0.0)
         brow = const.tile([P, H * P], BF16, name="brow")
         nc.vector.memset(brow[:], 0.0)
         nc.scalar.dma_start(out=brow[0:1, :], in_=bias.rearrange("(o h) c -> o (h c)", o=1))
@@ -247,16 +245,9 @@ def tile_multiheadhomogeneousattention_pa_kernel(tc, x, w_now, w_back1, w_back2,
             nc.tensor.matmul(out=bp[:], lhsT=ones[:], rhs=brow[:, 512 * half : 512 * (half + 1)], start=True, stop=True)
             nc.scalar.copy(out=bias_sb[:, 4 * half : 4 * half + 4, :].rearrange("p h c -> p (h c)"), in_=bp[:])
 
-        def stage_dummy(count):
-            dps = accp.tile([P, 512], F32, name="acc", tag="acc")
-            for i in range(count):
-                nc.tensor.matmul(out=dps[:], lhsT=ones[:], rhs=dz[:], start=(i == 0), stop=(i == count - 1))
-
         for item in PLAN.split():
             f = item.split(":")
-            if f[0][0] == "D" and len(f) == 1:
-                stage_dummy(int(f[0][1:]))
-            elif f[0][0] == "B" and len(f) == 1:
+            if f[0][0] == "B" and len(f) == 1:
                 stage_bias(int(f[0][1:]))
             elif f[0] == "R":
                 stage_r(f[1], int(f[2]) if len(f) > 2 else 1)

@@ -23,8 +23,8 @@ SPLIT = {"x00":4,"x01":4,"w3":2,"w4":2,"w5":2}
 PLAN = """
 T:x00:d Q:x00 T:x01:d Q:x01 T:w3:d Q:w3 S:0 T:w4:d Q:w4 T:w5:d B0 B1 Q:w5 T:x10:d Q:x10 T:x11:d R:w0 Q:x11 R:w1 S:1
 M:C01 M:C00 A:C01 T:w0 T:w1 A:C00 F:C0 R:w2 R:w6
-M:C10 Q:w0 M:C11 A:C10 Q:w1 T:w2 T:w6 A:C11 F:C1 R:w7
-M:A00 M:A01 A:A00 M:A10 A:A01 F:A0 M:A11 A:A10 Q:w2 T:w7 A:A11 F:A1 Q:w6
+M:C11 Q:w0 M:C10 A:C11 Q:w1 T:w2 T:w6 A:C10 F:C1 R:w7
+M:A00 Q:w2 M:A01 A:A00 M:A10 A:A01 F:A0 M:A11 A:A10 Q:w6 T:w7 A:A11 F:A1
 M:B00 M:B01 A:B00 Q:w7 M:B10 A:B01 F:B0 M:B11 A:B10 M:D0 A:B11 F:B1 M:D1 A:D0 F:D0 M:E0 A:D1 F:D1 M:E1a A:E0 F:E0 M:E1b A:E1a F:E1a A:E1b F:E1b:V
 """
 

@@ -21,7 +21,7 @@ LOAD_ORDER = ["x00","x01","w3","w4","w5","x10","x11","w0","w1","w2","w6","w7"]
 SPLIT = {"x00":4,"x01":4,"w3":2,"w4":2,"w5":2}
 
 PLAN = """
-T:x00:d Q:x00 T:x01:d Q:x01 T:w3:d Q:w3 S:0 T:w4:d Q:w4 T:w5:d B0 B1 Q:w5 T:x10:d Q:x10 T:x11:d R:w0 Q:x11 R:w1 S:1
+T:x00:d Q:x00 T:x01:d Q:x01 T:w3:d Q:w3 S:0 T:w4:d Q:w4 T:w5:d B0 B1 Q:w5 T:x10:d R:w0 Q:x10 T:x11:d R:w1 Q:x11 S:1
 M:C01 M:C00 A:C01 T:w0 T:w1 A:C00 F:C0 R:w2 R:w6
 M:C11 Q:w0 M:C10 A:C11 Q:w1 T:w2 T:w6 A:C10 F:C1 R:w7
 M:A00 Q:w2 M:A01 A:A00 M:A10 A:A01 F:A0 M:A11 A:A10 Q:w6 T:w7 A:A11 F:A1

@@ -93,12 +93,13 @@ def tile_multiheadhomogeneousattention_pa_kernel(tc, x, w_now, w_back1, w_back2,
 
         cod = {}
         sca = {}
-        for name in LOAD_ORDER:
-            cod[name] = codes.tile([P, 512], I32, name="c_" + name, align_bytes=64)
-            sca[name] = codes.tile([P, 512], U8, name="s_" + name, align_bytes=64)
+        for name in LOAD_ORDER + ["sh0", "sh1"]:
+            cpad, spad = (0, 64) if name[0] == "w" else (32, 192)
+            ct = codes.tile([P, 512 + cpad], I32, name="c_" + name, align_bytes=256)
+            st = codes.tile([P, 512 + spad], U8, name="s_" + name, align_bytes=256)
+            cod[name] = ct[:, cpad : cpad + 512]
+            sca[name] = st[:, spad : spad + 512]
         for n in range(B):
-            cod["sh%d" % n] = codes.tile([P, 512], I32, name="c_sh%d" % n, align_bytes=64)
-            sca["sh%d" % n] = codes.tile([P, 512], U8, name="s_sh%d" % n, align_bytes=64)
             nc.vector.memset(cod["sh%d" % n][:], 0)
             nc.vector.memset(sca["sh%d" % n][:].bitcast(I32), 0)
             nc.vector.memset(sca["x%d1" % n][:].bitcast(I32), 0)

from contextlib import ExitStack

import concourse.mybir as mybir
from concourse.masks import make_identity

B, S, D, P, H = 2, 512, 1024, 128, 8
FLOPS = 2 * B * S * D * P * 16

F32 = mybir.dt.float32
BF16 = mybir.dt.bfloat16
I32 = mybir.dt.int32
U8 = mybir.dt.uint8
FP8X4 = mybir.dt.float8_e4m3fn_x4
FP8 = mybir.dt.float8_e4m3fn
ALU = mybir.AluOpType
ACT = mybir.ActivationFunctionType

Y_SCALE = 140.0

LOAD_ORDER = ["x00","x01","w3","w4","w5","x10","x11","w0","w1","w2","w6","w7"]
SPLIT = {"x00":4,"x01":4,"w3":2,"w4":2,"w5":2}

PLAN = """
T:x00:d Q:x00 T:x01:d Q:x01 T:w3:d Q:w3 S:0 T:w4:d Q:w4 T:w5:d B0 B1 Q:w5 T:x10:d R:w0 Q:x10 T:x11:d R:w1 Q:x11 S:1
M:C01 M:C00 A:C01 T:w0 T:w1 A:C00 F:C0 R:w2 R:w6
M:C11 Q:w0 M:C10 A:C11 Q:w1 T:w2 T:w6 A:C10 F:C1 R:w7
M:A00 Q:w2 M:A01 A:A00 M:A10 A:A01 F:A0 M:A11 A:A10 Q:w6 T:w7 A:A11 F:A1
M:B00 M:B01 A:B00 Q:w7 M:B10 A:B01 F:B0 M:B11 A:B10 M:D0 A:B11 F:B1 M:D1 A:D0 F:D0 M:E0 A:D1 F:D1 M:E1a A:E0 F:E0 M:E1b A:E1a F:E1a A:E1b F:E1b:V
"""


def tile_multiheadhomogeneousattention_pa_kernel(tc, x, w_now, w_back1, w_back2, bias, out_0, out_1):
    nc = tc.nc
    with ExitStack() as ctx:
        const = ctx.enter_context(tc.tile_pool(name="const", bufs=1))
        raw = ctx.enter_context(tc.tile_pool(name="raw", bufs=1))
        codes = ctx.enter_context(tc.tile_pool(name="codes", bufs=1))
        grp = ctx.enter_context(tc.tile_pool(name="grp", bufs=4))
        reo = ctx.enter_context(tc.tile_pool(name="reo", bufs=4))
        outp = ctx.enter_context(tc.tile_pool(name="outp", bufs=1))
        f8p = ctx.enter_context(tc.tile_pool(name="f8p", bufs=6))
        tps = ctx.enter_context(tc.psum_pool(name="tps", bufs=4))
        accp = ctx.enter_context(tc.psum_pool(name="accp", bufs=4))
        ctx.enter_context(tc.manual_schedule())

        def xview(n, ap):
            return x[n].rearrange("(m a) k -> m a k", a=4)[:, 2 * ap : 2 * ap + 2, :]

        srcs = {
            "x00": [(xview(0, 0), 0, 2)],
            "x01": [(xview(0, 1), 0, 2)],
            "x10": [(xview(1, 0), 0, 2)],
            "x11": [(xview(1, 1), 0, 2)],
            "w0": [(w_now[0:2].rearrange("h c k -> c h k"), 0, 2)],
            "w1": [(w_now[3:5].rearrange("h c k -> c h k"), 0, 2)],
            "w2": [(w_back1[0:2].rearrange("h c k -> c h k"), 0, 2)],
            "w3": [(w_now[5:7].rearrange("h c k -> c h k"), 0, 2)],
            "w4": [(w_back1[2:4].rearrange("h c k -> c h k"), 0, 2)],
            "w5": [(w_back2[0:2].rearrange("h c k -> c h k"), 0, 2)],
            "w6": [(w_now[2:8:5].rearrange("h c k -> c h k"), 0, 2)],
            "w7": [
                (w_back1[4:5].rearrange("h c k -> c h k"), 0, 1),
                (w_back2[2:3].rearrange("h c k -> c h k"), 1, 1),
            ],
        }

        ones = const.tile([P, P], BF16, name="ones")
        nc.gpsimd.memset(ones[:], 1.0)
        brow = const.tile([P, H * P], BF16, name="brow")
        nc.vector.memset(brow[:], 0.0)
        nc.scalar.dma_start(out=brow[0:1, :], in_=bias.rearrange("(o h) c -> o (h c)", o=1))
        warm = const.tile([P, 1], F32, name="warm")
        warm2 = const.tile([P, 1], F32, name="warm2")
        nc.vector.memset(warm[:], 0.0)
        nc.scalar.activation(out=warm2[:], in_=warm[:], func=ACT.Copy, scale=1.0)
        ident = const.tile([P, P], F32, name="ident")
        make_identity(nc, ident[:])
        bias_sb = const.tile([P, H, P], F32, name="bias_sb")

        rawt = {}
        for name in LOAD_ORDER:
            t = raw.tile([P, 2, D], BF16, name="raw_" + name)
            rawt[name] = t
            parts = SPLIT.get(name, 1)
            for (view, i0, ni) in srcs[name]:
                if parts == 1:
                    nc.sync.dma_start(out=t[:, i0 : i0 + ni, :], in_=view)
                else:
                    for i in range(ni):
                        for g in range(parts // 2):
                            w = D // (parts // 2)
                            nc.sync.dma_start(out=t[:, i0 + i, g * w : (g + 1) * w], in_=view[:, i, g * w : (g + 1) * w])

        cod = {}
        sca = {}
        for name in LOAD_ORDER + ["sh0", "sh1"]:
            cpad, spad = (0, 64) if name[0] == "w" else (32, 192)
            ct = codes.tile([P, 512 + cpad], I32, name="c_" + name, align_bytes=256)
            st = codes.tile([P, 512 + spad], U8, name="s_" + name, align_bytes=256)
            cod[name] = ct[:, cpad : cpad + 512]
            sca[name] = st[:, spad : spad + 512]
        for n in range(B):
            nc.vector.memset(cod["sh%d" % n][:], 0)
            nc.vector.memset(sca["sh%d" % n][:].bitcast(I32), 0)
            nc.vector.memset(sca["x%d1" % n][:].bitcast(I32), 0)

        reot = {}
        grpt = {}

        def stage_r(name, pieces=1):
            r_t = reo.tile([P, 2, 512], F32, name="r_t", tag="r")
            reot[name] = r_t
            words = rawt[name][:].rearrange("p i k -> p (i k)").bitcast(F32)
            w = 512 // pieces
            for q in range(pieces):
                nc.vector.tensor_copy(
                    out=r_t[:, :, q * w : (q + 1) * w],
                    in_=words[:, 2 * q * w : 2 * (q + 1) * w].rearrange("p (m u) -> p u m", u=2),
                )

        def stage_q(name):
            nc.vector.quantize_mx(out=cod[name][:].bitcast(FP8X4), scales=sca[name][:], in_=grpt[name][:])

        def stage_s(n):
            if True:
                sh = "sh%d" % n
                name = "x%d1" % n
                nc.vector.tensor_copy(
                    out=cod[sh][:].rearrange("p (b m) -> p b m", b=4)[:, :, 1:P],
                    in_=cod[name][:].rearrange("p (b m) -> p b m", b=4)[:, :, 0 : P - 1],
                )
                nc.vector.tensor_copy(
                    out=sca[sh][:].rearrange("p (b m) -> p b m", b=4)[:, :, 1:P],
                    in_=sca[name][:].rearrange("p (b m) -> p b m", b=4)[:, :, 0 : P - 1],
                )

        def stage_t(name, direct, engines):
            g_t = grp.tile([P, 2048], BF16, name="g_t", tag="g", align_bytes=64)
            grpt[name] = g_t
            gw = g_t[:].bitcast(F32)
            if name[0] == "x":
                gv = gw.rearrange("p (i g m u) -> p i g m u", i=2, g=2, u=2)
            else:
                gv = gw.rearrange("p (g i m u) -> p i g m u", i=2, g=2, u=2)
            for i in range(2):
                pt = tps.tile([P, 4, P], F32, name="pt", tag="pt")
                for g in range(2):
                    for u in range(2):
                        if direct:
                            src = rawt[name][:, i, :].bitcast(F32)[:, 256 * g + u : 256 * (g + 1) : 2]
                        else:
                            src = reot[name][:, u, (2 * i + g) * P : (2 * i + g + 1) * P]
                        nc.tensor.transpose(pt[:, 2 * g + u, :], src, ident[:])
                if engines[i] == "S":
                    nc.scalar.copy(out=gv[:, i], in_=pt[:].rearrange("p (g u) m -> p g m u", u=2))
                else:
                    nc.vector.tensor_copy(out=gv[:, i], in_=pt[:].rearrange("p (g u) m -> p g m u", u=2))

        def lhs(n, a, j, g):
            s = a - j
            if s >= 0:
                name = "x%d%d" % (n, s // 2)
                off = ((s % 2) * 2 + g) * P
            else:
                name = "sh%d" % n
                off = ((s + 2) * 2 + g) * P
            return cod[name][:, off : off + P].bitcast(FP8X4), sca[name][:, off : off + P]

        def mm_group(out, n, a, wl, width):
            passes = [(j, g) for j in range(len(wl)) for g in range(2)]
            for idx, (j, g) in enumerate(passes):
                lc, ls = lhs(n, a, j, g)
                wn, wo = wl[j]
                c0 = 256 * g + wo
                nc.tensor.matmul_mx(
                    out=out,
                    lhsT=lc,
                    lhsT_scale=ls,
                    rhs=cod[wn][:, c0 : c0 + width].bitcast(FP8X4),
                    rhs_scale=sca[wn][:, c0 : c0 + width],
                    start=(idx == 0),
                    stop=(idx == len(passes) - 1),
                )

        def dview(dst, n, hsl, a0, na):
            return dst[n, hsl].rearrange("h (m a) c -> m h a c", a=4)[:, :, a0 : a0 + na, :].rearrange("m h a c -> m h (a c)")

        KIND = {
            "A": (0, 2, [("w0", 0)]),
            "B": (3, 2, [("w1", 0), ("w2", 0)]),
            "C": (5, 2, [("w3", 0), ("w4", 0), ("w5", 0)]),
            "D": (2, 1, [("w6", 0)]),
            "E": (7, 1, [("w6", P), ("w7", 0), ("w7", P)]),
        }
        otile = {}
        accs = {}

        def block_range(b):
            k = b[0]
            if KIND[k][1] == 2:
                return 2 * int(b[2]), 2
            if len(b) == 2:
                return 0, 4
            return {"a": (0, 2), "b": (2, 2), "c": (2, 1), "d": (3, 1)}[b[2]]

        def stage_m(b):
            h0, nh, wl = KIND[b[0]]
            n = int(b[1])
            a0, na = block_range(b)
            acc = accp.tile([P, na, nh * P], F32, name="acc", tag="acc")
            accs[b] = acc
            for ai in range(na):
                mm_group(acc[:, ai, :], n, a0 + ai, wl, nh * P)

        def stage_a(b):
            h0, nh, wl = KIND[b[0]]
            a0, na = block_range(b)
            key = b[0:2]
            if key not in otile:
                otile[key] = outp.tile([P, nh, 4, P], F32, name="o_" + key)
            o = otile[key]
            nc.vector.tensor_tensor(
                out=o[:, :, a0 : a0 + na, :],
                in0=accs[b][:].rearrange("p a (h c) -> p h a c", h=nh),
                in1=bias_sb[:, h0 : h0 + nh, :].unsqueeze(2).to_broadcast([P, nh, na, P]),
                op=ALU.add,
            )

        def stage_f(b, engine):
            h0, nh, wl = KIND[b[0]]
            n = int(b[1])
            a0, na = (0, 4) if len(b) == 2 else block_range(b)
            o_view = otile[b[0:2]][:, :, a0 : a0 + na, :].rearrange("p h a c -> p h (a c)")
            hsl = slice(h0, h0 + nh)
            f8 = f8p.tile([P, nh * na * P], FP8, name="f8", tag="f8")
            nc.sync.dma_start(out=dview(out_0, n, hsl, a0, na), in_=o_view)
            flat = o_view.rearrange("p h x -> p (h x)")
            if engine == "S":
                nc.scalar.activation(out=f8[:], in_=flat, func=ACT.Copy, scale=Y_SCALE, saturate=False)
            else:
                nc.vector.tensor_scalar(out=f8[:], in0=flat, scalar1=Y_SCALE, scalar2=None, op0=ALU.mult, saturate=False)
            nc.sync.dma_start(out=dview(out_1, n, hsl, a0, na), in_=f8[:].bitcast(U8).rearrange("p (h x) -> p h x", h=nh))

        def stage_bias(half):
            bp = accp.tile([P, 512], F32, name="acc", tag="acc")
            nc.tensor.matmul(out=bp[:], lhsT=ones[:], rhs=brow[:, 512 * half : 512 * (half + 1)], start=True, stop=True)
            nc.scalar.copy(out=bias_sb[:, 4 * half : 4 * half + 4, :].rearrange("p h c -> p (h c)"), in_=bp[:])

        for item in PLAN.split():
            f = item.split(":")
            if f[0][0] == "B" and len(f) == 1:
                stage_bias(int(f[0][1:]))
            elif f[0] == "R":
                stage_r(f[1], int(f[2]) if len(f) > 2 else 1)
            elif f[0] == "T":
                opts = f[2] if len(f) > 2 else ""
                stage_t(f[1], "d" in opts, "SV" if "v" in opts else "SS")
            elif f[0] == "Q":
                stage_q(f[1])
            elif f[0] == "S":
                stage_s(int(f[1]))
            elif f[0] == "M":
                stage_m(f[1])
            elif f[0] == "A":
                stage_a(f[1])
            elif f[0] == "F":
                stage_f(f[1], f[2] if len(f) > 2 else "S")
